import numpy as np
import ml_dtypes


def mxq(x, axis, fmt="e4m3"):
    dtype, down = {"e4m3": (ml_dtypes.float8_e4m3fn, 7), "e5m2": (ml_dtypes.float8_e5m2, 14)}[fmt]
    v = np.moveaxis(np.asarray(x, np.float32).astype(ml_dtypes.bfloat16).astype(np.float64), axis, -1)
    blocks = v.reshape(v.shape[:-1] + (-1, 32))
    amax = np.abs(blocks).max(-1, keepdims=True)
    byte = np.maximum(np.where(amax > 0, np.frexp(amax)[1] - 1 + 127, 0) - down, 1)
    scale = np.exp2(byte - 127.0)
    codes = (blocks / scale).astype(np.float32).astype(dtype).astype(np.float64)
    return np.moveaxis((codes * scale).reshape(v.shape), -1, axis)


WIDE = False


def mx_kscale(k):
    if not WIDE:
        return np.ones(k)
    levels = np.array([10, -10, 5, -5, 0])
    a = np.random.permutation(np.resize(levels, k // 512 * 4)).reshape(k // 512, 4)
    idx = np.arange(k)
    return np.exp2(a[idx // 512, idx % 128 // 32])


BF16 = ml_dtypes.bfloat16


def bf(x):
    return np.asarray(x, np.float32).astype(BF16)


def f64(x):
    return np.asarray(x).astype(np.float64)


B, S, D, H, DH = 2, 256, 2048, 16, 128
E = H * DH
EPS = 1e-6
MU = 0.5


def setup_inputs():
    s = mx_kscale(D)
    g = np.random.standard_normal((D, H, DH))
    g = (g - g.mean(-1, keepdims=True)) / np.sqrt(D * (1.0 + MU * MU))
    lev = 2.5 + np.random.random((1, H, 1))
    w = (g + lev / (D * MU * DH)).reshape(D, E)
    x = np.random.standard_normal((B, S, D)) + MU
    return {"x": bf(x * s), "w": bf(w / s[:, None])}


def reference(x, w):
    y = mxq(f64(x), 2, "e4m3") @ mxq(f64(w), 0, "e4m3")
    yh = y.reshape(B, S, H, DH).transpose(0, 2, 1, 3)
    return yh / (yh.sum(-1, keepdims=True) + EPS)

@@ -1,0 +1,152 @@
+import concourse.mybir as mybir
+from concourse.masks import make_identity
+
+F32 = mybir.dt.float32
+BF16 = mybir.dt.bfloat16
+U32 = mybir.dt.uint32
+U8 = mybir.dt.uint8
+FP8X4 = mybir.dt.float8_e4m3fn_x4
+COPY = mybir.ActivationFunctionType.Copy
+
+P = 128
+PACK = 4
+K_PASS = P * PACK
+B, S, D, H, DH = 2, 256, 2048, 16, 128
+EPS = 1e-6
+PASSES = D // K_PASS
+TOKEN_TILES = S // P
+GROUP_HEADS = 4
+GROUP_COLS = GROUP_HEADS * DH
+GROUPS = H // GROUP_HEADS
+WORDS = K_PASS // 2
+VECTOR_COLS = 320
+
+FLOPS = 2 * B * S * D * H * DH
+
+
+def tile_multiheadattention_pa_kernel(tc, x, w, out):
+    nc = tc.nc
+    with tc.tile_pool(name="keep", bufs=1) as keep, tc.tile_pool(name="stage", bufs=4) as stage, tc.psum_pool(
+        name="psum", bufs=8
+    ) as psum:
+        ident = keep.tile([P, P], F32)
+        make_identity(nc, ident[:])
+
+        x_raw = keep.tile([P, B * TOKEN_TILES * D], BF16)
+        x_rows = x_raw[:].rearrange("p (b m k) -> p b m k", b=B, m=TOKEN_TILES)
+        x_words = x_raw[:].bitcast(F32).rearrange("p (b m q) -> p b m q", b=B, m=TOKEN_TILES)
+        x_grouped = keep.tile([P, B * PASSES * S * PACK], BF16, align_bytes=64)
+        x_grouped_cols = x_grouped[:].rearrange("p (b c) -> p b c", b=B)
+        x_grouped_words = x_grouped[:].bitcast(F32).rearrange(
+            "p (b g m r u) -> p b g m r u", b=B, g=PASSES, m=TOKEN_TILES, u=2
+        )
+        x_codes = keep.tile([P, B, PASSES * S], U32, align_bytes=64)
+        x_scales = keep.tile([P, B, PASSES * S], U8, align_bytes=64)
+
+        w_raw = keep.tile([P, GROUPS, PASSES, PACK, GROUP_COLS], BF16)
+        w_codes = keep.tile([P, GROUPS, PASSES, GROUP_COLS], U32, align_bytes=64)
+        w_scales = keep.tile([P, GROUPS, PASSES, GROUP_COLS], U8, align_bytes=64)
+
+        def load_w(c, g):
+            for u in range(2):
+                k0 = K_PASS * g + 2 * P * u
+                nc.sync.dma_start(
+                    out=w_raw[:, c, g, 2 * u : 2 * u + 2, :],
+                    in_=w[k0 : k0 + 2 * P, GROUP_COLS * c : GROUP_COLS * (c + 1)].rearrange("(p e) n -> p e n", e=2),
+                )
+
+        def load_x(b):
+            nc.sync.dma_start(out=x_rows[:, b], in_=x[b].rearrange("(p m) k -> p m k", m=TOKEN_TILES))
+
+        def quantise_x(b):
+            for g in range(PASSES):
+                xt = psum.tile([P, TOKEN_TILES, 2, P], F32, tag="bank")
+                for m in range(TOKEN_TILES):
+                    for u in range(2):
+                        q0 = WORDS * g + P * u
+                        nc.tensor.transpose(xt[:, m, u, :], x_words[:, b, m, q0 : q0 + P], ident[:])
+                planes = xt[:].rearrange("p m u r -> p m r u")
+                if g % 2 == 0:
+                    nc.scalar.copy(out=x_grouped_words[:, b, g], in_=planes)
+                else:
+                    nc.vector.tensor_copy(out=x_grouped_words[:, b, g], in_=planes)
+            nc.vector.quantize_mx(out=x_codes[:, b, :].bitcast(FP8X4), scales=x_scales[:, b, :], in_=x_grouped_cols[:, b, :])
+
+        def regroup_w(c, g):
+            grouped = stage.tile([P, GROUP_COLS, PACK], BF16, align_bytes=64, tag="grouped")
+            dst = grouped[:].rearrange("p (c i) t -> p c t i", i=4)
+            src = w_raw[:, c, g].rearrange("p t (c i) -> p c t i", i=4)
+            split = VECTOR_COLS // 4
+            nc.vector.tensor_copy(out=dst[:, :split], in_=src[:, :split])
+            nc.scalar.copy(out=dst[:, split:], in_=src[:, split:])
+            return grouped
+
+        def quantise_w(c, g, grouped):
+            nc.vector.quantize_mx(
+                out=w_codes[:, c, g, :].bitcast(FP8X4),
+                scales=w_scales[:, c, g, :],
+                in_=grouped[:].rearrange("p n t -> p (n t)"),
+            )
+
+        def multiply(c, g, banks):
+            for b in range(B):
+                for m in range(TOKEN_TILES):
+                    tokens = slice(S * g + P * m, S * g + P * (m + 1))
+                    nc.tensor.matmul_mx(
+                        out=banks[b][m][:],
+                        lhsT=x_codes[:, b, tokens].bitcast(FP8X4),
+                        lhsT_scale=x_scales[:, b, tokens],
+                        rhs=w_codes[:, c, g, :].bitcast(FP8X4),
+                        rhs_scale=w_scales[:, c, g, :],
+                        start=(g == 0),
+                        stop=(g == PASSES - 1),
+                    )
+
+        def normalise_and_store(c, banks):
+            y = stage.tile([P, B, GROUP_HEADS, TOKEN_TILES, DH], F32, tag="y")
+            sums = stage.tile([P, B, TOKEN_TILES, GROUP_HEADS], F32, tag="sums")
+            inverse = stage.tile([P, B, TOKEN_TILES, GROUP_HEADS], F32, tag="inverse")
+            for b in range(B):
+                for m in range(TOKEN_TILES):
+                    for h in range(GROUP_HEADS):
+                        nc.scalar.activation(
+                            out=y[:, b, h, m, :],
+                            in_=banks[b][m][:, DH * h : DH * (h + 1)],
+                            func=COPY,
+                            accum_out=sums[:, b, m, h : h + 1],
+                        )
+                nc.vector.tensor_scalar_add(out=inverse[:, b], in0=sums[:, b], scalar1=EPS)
+                nc.vector.reciprocal(out=inverse[:, b], in_=inverse[:, b])
+                for m in range(TOKEN_TILES):
+                    for h in range(GROUP_HEADS):
+                        nc.vector.tensor_scalar_mul(
+                            out=y[:, b, h, m, :], in0=y[:, b, h, m, :], scalar1=inverse[:, b, m, h : h + 1]
+                        )
+                nc.sync.dma_start(
+                    out=out[b, GROUP_HEADS * c : GROUP_HEADS * (c + 1)].rearrange("h (p m) d -> p h (m d)", m=TOKEN_TILES),
+                    in_=y[:, b].rearrange("p h m d -> p h (m d)"),
+                )
+
+        chunks = [(c, g) for c in range(GROUPS) for g in range(PASSES)]
+        load_w(0, 0)
+        for b in range(B):
+            load_x(b)
+        for c, g in chunks[1:]:
+            load_w(c, g)
+
+        grouped_now = regroup_w(0, 0)
+        for b in range(B):
+            quantise_x(b)
+        banks = []
+        for j, (c, g) in enumerate(chunks):
+            grouped_next = regroup_w(*chunks[j + 1]) if j + 1 < len(chunks) else None
+            quantise_w(c, g, grouped_now)
+            if g == 0:
+                banks = [
+                    [psum.tile([P, GROUP_COLS], F32, tag="bank", name="acc") for m in range(TOKEN_TILES)]
+                    for b in range(B)
+                ]
+            multiply(c, g, banks)
+            if g == PASSES - 1:
+                normalise_and_store(c, banks)
+            grouped_now = grouped_next

@@ -1,3 +1,5 @@
+from contextlib import ExitStack
+
 import concourse.mybir as mybir
 from concourse.masks import make_identity
 
@@ -18,17 +20,23 @@ TOKEN_TILES = S // P
 GROUP_HEADS = 4
 GROUP_COLS = GROUP_HEADS * DH
 GROUPS = H // GROUP_HEADS
+GROUP_BANKS = B * TOKEN_TILES
+SUM_LAG = PASSES
 WORDS = K_PASS // 2
-VECTOR_COLS = 320
+VECTOR_COLS = 304
 
 FLOPS = 2 * B * S * D * H * DH
 
 
 def tile_multiheadattention_pa_kernel(tc, x, w, out):
     nc = tc.nc
-    with tc.tile_pool(name="keep", bufs=1) as keep, tc.tile_pool(name="stage", bufs=4) as stage, tc.psum_pool(
-        name="psum", bufs=8
-    ) as psum:
+    with ExitStack() as ctx:
+        keep = ctx.enter_context(tc.tile_pool(name="keep", bufs=1))
+        stage = ctx.enter_context(tc.tile_pool(name="stage", bufs=3))
+        results = ctx.enter_context(tc.tile_pool(name="results", bufs=GROUPS))
+        psum = ctx.enter_context(tc.psum_pool(name="psum", bufs=1))
+        ctx.enter_context(tc.manual_schedule())
+
         ident = keep.tile([P, P], F32)
         make_identity(nc, ident[:])
 
@@ -47,6 +55,9 @@ def tile_multiheadattention_pa_kernel(tc, x, w, out):
         w_codes = keep.tile([P, GROUPS, PASSES, GROUP_COLS], U32, align_bytes=64)
         w_scales = keep.tile([P, GROUPS, PASSES, GROUP_COLS], U8, align_bytes=64)
 
+        def bank(index, shape, name):
+            return psum.tile(shape, F32, tag="bank%d" % index, name=name)
+
         def load_w(c, g):
             for u in range(2):
                 k0 = K_PASS * g + 2 * P * u
@@ -56,97 +67,117 @@ def tile_multiheadattention_pa_kernel(tc, x, w, out):
                 )
 
         def load_x(b):
-            nc.sync.dma_start(out=x_rows[:, b], in_=x[b].rearrange("(p m) k -> p m k", m=TOKEN_TILES))
+            for half in range(2):
+                k_half = slice(D // 2 * half, D // 2 * (half + 1))
+                nc.sync.dma_start(
+                    out=x_rows[:, b, :, k_half], in_=x[b, :, k_half].rearrange("(p m) k -> p m k", m=TOKEN_TILES)
+                )
 
         def quantise_x(b):
             for g in range(PASSES):
-                xt = psum.tile([P, TOKEN_TILES, 2, P], F32, tag="bank")
+                xt = bank(GROUP_BANKS * b + g, [P, TOKEN_TILES, 2, P], "xt")
                 for m in range(TOKEN_TILES):
                     for u in range(2):
                         q0 = WORDS * g + P * u
                         nc.tensor.transpose(xt[:, m, u, :], x_words[:, b, m, q0 : q0 + P], ident[:])
-                planes = xt[:].rearrange("p m u r -> p m r u")
-                if g % 2 == 0:
-                    nc.scalar.copy(out=x_grouped_words[:, b, g], in_=planes)
-                else:
-                    nc.vector.tensor_copy(out=x_grouped_words[:, b, g], in_=planes)
-            nc.vector.quantize_mx(out=x_codes[:, b, :].bitcast(FP8X4), scales=x_scales[:, b, :], in_=x_grouped_cols[:, b, :])
+                nc.scalar.copy(out=x_grouped_words[:, b, g], in_=xt[:].rearrange("p m u r -> p m r u"))
+                nc.vector.quantize_mx(
+                    out=x_codes[:, b, S * g : S * (g + 1)].bitcast(FP8X4),
+                    scales=x_scales[:, b, S * g : S * (g + 1)],
+                    in_=x_grouped_cols[:, b, S * PACK * g : S * PACK * (g + 1)],
+                )
+
+        grouped = {}
 
         def regroup_w(c, g):
-            grouped = stage.tile([P, GROUP_COLS, PACK], BF16, align_bytes=64, tag="grouped")
-            dst = grouped[:].rearrange("p (c i) t -> p c t i", i=4)
+            grouped[(c, g)] = stage.tile([P, GROUP_COLS, PACK], BF16, align_bytes=64, tag="grouped", name="grouped")
+            dst = grouped[(c, g)][:].rearrange("p (c i) t -> p c t i", i=4)
             src = w_raw[:, c, g].rearrange("p t (c i) -> p c t i", i=4)
             split = VECTOR_COLS // 4
             nc.vector.tensor_copy(out=dst[:, :split], in_=src[:, :split])
             nc.scalar.copy(out=dst[:, split:], in_=src[:, split:])
-            return grouped
 
-        def quantise_w(c, g, grouped):
+        def quantise_w(c, g):
             nc.vector.quantize_mx(
                 out=w_codes[:, c, g, :].bitcast(FP8X4),
                 scales=w_scales[:, c, g, :],
-                in_=grouped[:].rearrange("p n t -> p (n t)"),
+                in_=grouped[(c, g)][:].rearrange("p n t -> p (n t)"),
             )
 
-        def multiply(c, g, banks):
-            for b in range(B):
-                for m in range(TOKEN_TILES):
-                    tokens = slice(S * g + P * m, S * g + P * (m + 1))
-                    nc.tensor.matmul_mx(
-                        out=banks[b][m][:],
-                        lhsT=x_codes[:, b, tokens].bitcast(FP8X4),
-                        lhsT_scale=x_scales[:, b, tokens],
-                        rhs=w_codes[:, c, g, :].bitcast(FP8X4),
-                        rhs_scale=w_scales[:, c, g, :],
-                        start=(g == 0),
-                        stop=(g == PASSES - 1),
-                    )
+        acc = {}
 
-        def normalise_and_store(c, banks):
-            y = stage.tile([P, B, GROUP_HEADS, TOKEN_TILES, DH], F32, tag="y")
-            sums = stage.tile([P, B, TOKEN_TILES, GROUP_HEADS], F32, tag="sums")
-            inverse = stage.tile([P, B, TOKEN_TILES, GROUP_HEADS], F32, tag="inverse")
-            for b in range(B):
-                for m in range(TOKEN_TILES):
-                    for h in range(GROUP_HEADS):
-                        nc.scalar.activation(
-                            out=y[:, b, h, m, :],
-                            in_=banks[b][m][:, DH * h : DH * (h + 1)],
-                            func=COPY,
-                            accum_out=sums[:, b, m, h : h + 1],
-                        )
-                nc.vector.tensor_scalar_add(out=inverse[:, b], in0=sums[:, b], scalar1=EPS)
-                nc.vector.reciprocal(out=inverse[:, b], in_=inverse[:, b])
-                for m in range(TOKEN_TILES):
-                    for h in range(GROUP_HEADS):
-                        nc.vector.tensor_scalar_mul(
-                            out=y[:, b, h, m, :], in0=y[:, b, h, m, :], scalar1=inverse[:, b, m, h : h + 1]
-                        )
-                nc.sync.dma_start(
-                    out=out[b, GROUP_HEADS * c : GROUP_HEADS * (c + 1)].rearrange("h (p m) d -> p h (m d)", m=TOKEN_TILES),
-                    in_=y[:, b].rearrange("p h m d -> p h (m d)"),
+        def multiply(c, g, b):
+            for m in range(TOKEN_TILES):
+                if g == 0:
+                    acc[(c, b, m)] = bank(GROUP_BANKS * (c % 2) + TOKEN_TILES * b + m, [P, GROUP_COLS], "acc")
+                tokens = slice(S * g + P * m, S * g + P * (m + 1))
+                nc.tensor.matmul_mx(
+                    out=acc[(c, b, m)][:],
+                    lhsT=x_codes[:, b, tokens].bitcast(FP8X4),
+                    lhsT_scale=x_scales[:, b, tokens],
+                    rhs=w_codes[:, c, g, :].bitcast(FP8X4),
+                    rhs_scale=w_scales[:, c, g, :],
+                    start=(g == 0),
+                    stop=(g == PASSES - 1),
                 )
 
+        y = {}
+        sums = {}
+        inverse = {}
+
+        def sum_heads(c, b, m):
+            if b == 0 and m == 0:
+                y[c] = results.tile([P, B, GROUP_HEADS, TOKEN_TILES, DH], F32, tag="y", name="y")
+                sums[c] = results.tile([P, B, TOKEN_TILES, GROUP_HEADS], F32, tag="sums", name="sums")
+                inverse[c] = results.tile([P, B, TOKEN_TILES, GROUP_HEADS], F32, tag="inverse", name="inverse")
+            for h in range(GROUP_HEADS):
+                nc.scalar.activation(
+                    out=y[c][:, b, h, m, :],
+                    in_=acc[(c, b, m)][:, DH * h : DH * (h + 1)],
+                    func=COPY,
+                    accum_out=sums[c][:, b, m, h : h + 1],
+                )
+
+        def scale_and_store(c, b):
+            for m in range(TOKEN_TILES):
+                for h in range(GROUP_HEADS):
+                    nc.vector.tensor_scalar_mul(
+                        out=y[c][:, b, h, m, :], in0=y[c][:, b, h, m, :], scalar1=inverse[c][:, b, m, h : h + 1]
+                    )
+            nc.sync.dma_start(
+                out=out[b, GROUP_HEADS * c : GROUP_HEADS * (c + 1)].rearrange("h (p m) d -> p h (m d)", m=TOKEN_TILES),
+                in_=y[c][:, b].rearrange("p h m d -> p h (m d)"),
+            )
+
         chunks = [(c, g) for c in range(GROUPS) for g in range(PASSES)]
-        load_w(0, 0)
+        units = [(c, b, m) for c in range(GROUPS) for b in range(B) for m in range(TOKEN_TILES)]
+
         for b in range(B):
             load_x(b)
-        for c, g in chunks[1:]:
+        for c, g in chunks:
             load_w(c, g)
 
-        grouped_now = regroup_w(0, 0)
         for b in range(B):
             quantise_x(b)
-        banks = []
-        for j, (c, g) in enumerate(chunks):
-            grouped_next = regroup_w(*chunks[j + 1]) if j + 1 < len(chunks) else None
-            quantise_w(c, g, grouped_now)
-            if g == 0:
-                banks = [
-                    [psum.tile([P, GROUP_COLS], F32, tag="bank", name="acc") for m in range(TOKEN_TILES)]
-                    for b in range(B)
-                ]
-            multiply(c, g, banks)
-            if g == PASSES - 1:
-                normalise_and_store(c, banks)
-            grouped_now = grouped_next
+        regroup_w(0, 0)
+
+        for j in range(len(chunks) + SUM_LAG + 2):
+            summed = j - SUM_LAG - 1
+            finish = None
+            if 0 <= summed < len(units) and units[summed][2] == TOKEN_TILES - 1:
+                finish = units[summed][:2]
+            if finish:
+                nc.vector.tensor_scalar_add(out=inverse[finish[0]][:, finish[1]], in0=sums[finish[0]][:, finish[1]], scalar1=EPS)
+            if j < len(chunks):
+                c, g = chunks[j]
+                quantise_w(c, g)
+                for b in range(B):
+                    multiply(c, g, b)
+            if finish:
+                nc.vector.reciprocal(out=inverse[finish[0]][:, finish[1]], in_=inverse[finish[0]][:, finish[1]])
+            if j + 1 < len(chunks):
+                regroup_w(*chunks[j + 1])
+            if 0 <= j - SUM_LAG < len(units):
+                sum_heads(*units[j - SUM_LAG])
+            if finish:
+                scale_and_store(*finish)

@@ -73,19 +73,22 @@ def tile_multiheadattention_pa_kernel(tc, x, w, out):
                     out=x_rows[:, b, :, k_half], in_=x[b, :, k_half].rearrange("(p m) k -> p m k", m=TOKEN_TILES)
                 )
 
-        def quantise_x(b):
-            for g in range(PASSES):
-                xt = bank(GROUP_BANKS * b + g, [P, TOKEN_TILES, 2, P], "xt")
-                for m in range(TOKEN_TILES):
-                    for u in range(2):
-                        q0 = WORDS * g + P * u
-                        nc.tensor.transpose(xt[:, m, u, :], x_words[:, b, m, q0 : q0 + P], ident[:])
-                nc.scalar.copy(out=x_grouped_words[:, b, g], in_=xt[:].rearrange("p m u r -> p m r u"))
-                nc.vector.quantize_mx(
-                    out=x_codes[:, b, S * g : S * (g + 1)].bitcast(FP8X4),
-                    scales=x_scales[:, b, S * g : S * (g + 1)],
-                    in_=x_grouped_cols[:, b, S * PACK * g : S * PACK * (g + 1)],
-                )
+        xt = {}
+
+        def turn_x(b, g):
+            xt[(b, g)] = bank(GROUP_BANKS * b + g, [P, TOKEN_TILES, 2, P], "xt")
+            for m in range(TOKEN_TILES):
+                for u in range(2):
+                    q0 = WORDS * g + P * u
+                    nc.tensor.transpose(xt[(b, g)][:, m, u, :], x_words[:, b, m, q0 : q0 + P], ident[:])
+
+        def quantise_x(b, g):
+            nc.scalar.copy(out=x_grouped_words[:, b, g], in_=xt[(b, g)][:].rearrange("p m u r -> p m r u"))
+            nc.vector.quantize_mx(
+                out=x_codes[:, b, S * g : S * (g + 1)].bitcast(FP8X4),
+                scales=x_scales[:, b, S * g : S * (g + 1)],
+                in_=x_grouped_cols[:, b, S * PACK * g : S * PACK * (g + 1)],
+            )
 
         grouped = {}
 
@@ -158,10 +161,15 @@ def tile_multiheadattention_pa_kernel(tc, x, w, out):
             load_w(c, g)
 
         for b in range(B):
-            quantise_x(b)
+            for g in range(PASSES):
+                turn_x(b, g)
+        for g in range(PASSES):
+            quantise_x(0, g)
         regroup_w(0, 0)
 
         for j in range(len(chunks) + SUM_LAG + 2):
+            if j < PASSES:
+                quantise_x(1, j)
             summed = j - SUM_LAG - 1
             finish = None
             if 0 <= summed < len(units) and units[summed][2] == TOKEN_TILES - 1:

from contextlib import ExitStack

import concourse.mybir as mybir
from concourse.masks import make_identity

F32 = mybir.dt.float32
BF16 = mybir.dt.bfloat16
U32 = mybir.dt.uint32
U8 = mybir.dt.uint8
FP8X4 = mybir.dt.float8_e4m3fn_x4
COPY = mybir.ActivationFunctionType.Copy

P = 128
PACK = 4
K_PASS = P * PACK
B, S, D, H, DH = 2, 256, 2048, 16, 128
EPS = 1e-6
PASSES = D // K_PASS
TOKEN_TILES = S // P
GROUP_HEADS = 4
GROUP_COLS = GROUP_HEADS * DH
GROUPS = H // GROUP_HEADS
GROUP_BANKS = B * TOKEN_TILES
SUM_LAG = PASSES
WORDS = K_PASS // 2
VECTOR_COLS = 304

FLOPS = 2 * B * S * D * H * DH


def tile_multiheadattention_pa_kernel(tc, x, w, out):
    nc = tc.nc
    with ExitStack() as ctx:
        keep = ctx.enter_context(tc.tile_pool(name="keep", bufs=1))
        stage = ctx.enter_context(tc.tile_pool(name="stage", bufs=3))
        results = ctx.enter_context(tc.tile_pool(name="results", bufs=GROUPS))
        psum = ctx.enter_context(tc.psum_pool(name="psum", bufs=1))
        ctx.enter_context(tc.manual_schedule())

        ident = keep.tile([P, P], F32)
        make_identity(nc, ident[:])

        x_raw = keep.tile([P, B * TOKEN_TILES * D], BF16)
        x_rows = x_raw[:].rearrange("p (b m k) -> p b m k", b=B, m=TOKEN_TILES)
        x_words = x_raw[:].bitcast(F32).rearrange("p (b m q) -> p b m q", b=B, m=TOKEN_TILES)
        x_grouped = keep.tile([P, B * PASSES * S * PACK], BF16, align_bytes=64)
        x_grouped_cols = x_grouped[:].rearrange("p (b c) -> p b c", b=B)
        x_grouped_words = x_grouped[:].bitcast(F32).rearrange(
            "p (b g m r u) -> p b g m r u", b=B, g=PASSES, m=TOKEN_TILES, u=2
        )
        x_codes = keep.tile([P, B, PASSES * S], U32, align_bytes=64)
        x_scales = keep.tile([P, B, PASSES * S], U8, align_bytes=64)

        w_raw = keep.tile([P, GROUPS, PASSES, PACK, GROUP_COLS], BF16)
        w_codes = keep.tile([P, GROUPS, PASSES, GROUP_COLS], U32, align_bytes=64)
        w_scales = keep.tile([P, GROUPS, PASSES, GROUP_COLS], U8, align_bytes=64)

        def bank(index, shape, name):
            return psum.tile(shape, F32, tag="bank%d" % index, name=name)

        def load_w(c, g):
            for u in range(2):
                k0 = K_PASS * g + 2 * P * u
                nc.sync.dma_start(
                    out=w_raw[:, c, g, 2 * u : 2 * u + 2, :],
                    in_=w[k0 : k0 + 2 * P, GROUP_COLS * c : GROUP_COLS * (c + 1)].rearrange("(p e) n -> p e n", e=2),
                )

        def load_x(b):
            for half in range(2):
                k_half = slice(D // 2 * half, D // 2 * (half + 1))
                nc.sync.dma_start(
                    out=x_rows[:, b, :, k_half], in_=x[b, :, k_half].rearrange("(p m) k -> p m k", m=TOKEN_TILES)
                )

        xt = {}

        def turn_x(b, g):
            xt[(b, g)] = bank(GROUP_BANKS * b + g, [P, TOKEN_TILES, 2, P], "xt")
            for m in range(TOKEN_TILES):
                for u in range(2):
                    q0 = WORDS * g + P * u
                    nc.tensor.transpose(xt[(b, g)][:, m, u, :], x_words[:, b, m, q0 : q0 + P], ident[:])

        def quantise_x(b, g):
            nc.scalar.copy(out=x_grouped_words[:, b, g], in_=xt[(b, g)][:].rearrange("p m u r -> p m r u"))
            nc.vector.quantize_mx(
                out=x_codes[:, b, S * g : S * (g + 1)].bitcast(FP8X4),
                scales=x_scales[:, b, S * g : S * (g + 1)],
                in_=x_grouped_cols[:, b, S * PACK * g : S * PACK * (g + 1)],
            )

        grouped = {}

        def regroup_w(c, g):
            grouped[(c, g)] = stage.tile([P, GROUP_COLS, PACK], BF16, align_bytes=64, tag="grouped", name="grouped")
            dst = grouped[(c, g)][:].rearrange("p (c i) t -> p c t i", i=4)
            src = w_raw[:, c, g].rearrange("p t (c i) -> p c t i", i=4)
            split = VECTOR_COLS // 4
            nc.vector.tensor_copy(out=dst[:, :split], in_=src[:, :split])
            nc.scalar.copy(out=dst[:, split:], in_=src[:, split:])

        def quantise_w(c, g):
            nc.vector.quantize_mx(
                out=w_codes[:, c, g, :].bitcast(FP8X4),
                scales=w_scales[:, c, g, :],
                in_=grouped[(c, g)][:].rearrange("p n t -> p (n t)"),
            )

        acc = {}

        def multiply(c, g, b):
            for m in range(TOKEN_TILES):
                if g == 0:
                    acc[(c, b, m)] = bank(GROUP_BANKS * (c % 2) + TOKEN_TILES * b + m, [P, GROUP_COLS], "acc")
                tokens = slice(S * g + P * m, S * g + P * (m + 1))
                nc.tensor.matmul_mx(
                    out=acc[(c, b, m)][:],
                    lhsT=x_codes[:, b, tokens].bitcast(FP8X4),
                    lhsT_scale=x_scales[:, b, tokens],
                    rhs=w_codes[:, c, g, :].bitcast(FP8X4),
                    rhs_scale=w_scales[:, c, g, :],
                    start=(g == 0),
                    stop=(g == PASSES - 1),
                )

        y = {}
        sums = {}
        inverse = {}

        def sum_heads(c, b, m):
            if b == 0 and m == 0:
                y[c] = results.tile([P, B, GROUP_HEADS, TOKEN_TILES, DH], F32, tag="y", name="y")
                sums[c] = results.tile([P, B, TOKEN_TILES, GROUP_HEADS], F32, tag="sums", name="sums")
                inverse[c] = results.tile([P, B, TOKEN_TILES, GROUP_HEADS], F32, tag="inverse", name="inverse")
            for h in range(GROUP_HEADS):
                nc.scalar.activation(
                    out=y[c][:, b, h, m, :],
                    in_=acc[(c, b, m)][:, DH * h : DH * (h + 1)],
                    func=COPY,
                    accum_out=sums[c][:, b, m, h : h + 1],
                )

        def scale_and_store(c, b):
            for m in range(TOKEN_TILES):
                for h in range(GROUP_HEADS):
                    nc.vector.tensor_scalar_mul(
                        out=y[c][:, b, h, m, :], in0=y[c][:, b, h, m, :], scalar1=inverse[c][:, b, m, h : h + 1]
                    )
            nc.sync.dma_start(
                out=out[b, GROUP_HEADS * c : GROUP_HEADS * (c + 1)].rearrange("h (p m) d -> p h (m d)", m=TOKEN_TILES),
                in_=y[c][:, b].rearrange("p h m d -> p h (m d)"),
            )

        chunks = [(c, g) for c in range(GROUPS) for g in range(PASSES)]
        units = [(c, b, m) for c in range(GROUPS) for b in range(B) for m in range(TOKEN_TILES)]

        for b in range(B):
            load_x(b)
        for c, g in chunks:
            load_w(c, g)

        for b in range(B):
            for g in range(PASSES):
                turn_x(b, g)
        for g in range(PASSES):
            quantise_x(0, g)
        regroup_w(0, 0)

        for j in range(len(chunks) + SUM_LAG + 2):
            if j < PASSES:
                quantise_x(1, j)
            summed = j - SUM_LAG - 1
            finish = None
            if 0 <= summed < len(units) and units[summed][2] == TOKEN_TILES - 1:
                finish = units[summed][:2]
            if finish:
                nc.vector.tensor_scalar_add(out=inverse[finish[0]][:, finish[1]], in0=sums[finish[0]][:, finish[1]], scalar1=EPS)
            if j < len(chunks):
                c, g = chunks[j]
                quantise_w(c, g)
                for b in range(B):
                    multiply(c, g, b)
            if finish:
                nc.vector.reciprocal(out=inverse[finish[0]][:, finish[1]], in_=inverse[finish[0]][:, finish[1]])
            if j + 1 < len(chunks):
                regroup_w(*chunks[j + 1])
            if 0 <= j - SUM_LAG < len(units):
                sum_heads(*units[j - SUM_LAG])
            if finish:
                scale_and_store(*finish)
